import numpy as np
import ml_dtypes

BF16 = ml_dtypes.bfloat16


def bf(x):
    return np.asarray(x, np.float32).astype(BF16)


def f32(x):
    return np.asarray(x, np.float32)


def f64(x):
    return np.asarray(x).astype(np.float64)


def striped(idx):
    return np.tile(idx.reshape(-1, 16).T, (8, 1))


C, V, B, T, H, DH, N = 768, 4096, 4, 256, 6, 128, 1024
EPS = 1e-5
NEG = -1000000000.0
BASE = 10000.0
QK = 1.5


def positions():
    i = np.arange(C)
    expo = (2 * (i // 2)).astype(np.float32) / np.float32(C)
    den = f32(np.power(BASE, f64(expo)))
    angle = np.arange(T, dtype=np.float32)[None, :] / den[:, None]
    return f32(np.where((i % 2 == 0)[:, None], np.sin(f64(angle)), np.cos(f64(angle))))


def heads(z):
    return z.reshape(H, DH, B, T).transpose(2, 0, 3, 1)


def setup_inputs():
    return {
        "embedding": f32(np.random.standard_normal((C, V))),
        "pos": positions(),
        "gamma": f32(1.0 + 0.1 * np.random.standard_normal((C, 1))),
        "beta": f32(0.1 * np.random.standard_normal((C, 1))),
        "wq": bf(QK * np.random.standard_normal((C, C)) / np.sqrt(C)),
        "wk": bf(QK * np.random.standard_normal((C, C)) / np.sqrt(C)),
        "wv": bf(np.random.standard_normal((C, C)) / np.sqrt(C)),
        "wo": bf(np.random.standard_normal((C, C)) / np.sqrt(C)),
        "offs": striped(np.random.permutation(np.tile(np.arange(V), 2))[:N]),
    }


def reference(embedding, pos, gamma, beta, wq, wk, wv, wo, offs):
    idx = offs[:16].T.reshape(-1)
    x = f64(embedding)[:, idx] + np.tile(f64(pos), (1, B))
    mean = x.mean(axis=0, keepdims=True)
    var = ((x - mean) ** 2).mean(axis=0, keepdims=True)
    h = f64(gamma) * ((x - mean) / np.sqrt(var + EPS)) + f64(beta)
    q = heads(f64(wq).T @ h)
    k = heads(f64(wk).T @ h)
    v = heads(f64(wv).T @ h)
    scores = (q @ k.transpose(0, 1, 3, 2)) / np.sqrt(DH)
    scores = np.where(np.triu(np.ones((T, T), bool), 1), NEG, scores)
    p = np.exp(scores - scores.max(axis=-1, keepdims=True))
    p = p / p.sum(axis=-1, keepdims=True)
    attn = (p @ v).transpose(1, 3, 0, 2).reshape(C, N)
    return x + f64(wo).T @ attn

@@ -1,0 +1,215 @@
+import math
+
+import concourse.mybir as mybir
+from concourse.masks import make_identity
+
+F32 = mybir.dt.float32
+BF16 = mybir.dt.bfloat16
+U16 = mybir.dt.uint16
+ALU = mybir.AluOpType
+ACT = mybir.ActivationFunctionType
+AXIS = mybir.AxisListType
+
+P = 128
+C, V, B, T, H, DH, N = 768, 4096, 4, 256, 6, 128, 1024
+CB = C // P
+HALF = 512
+SEQS = HALF // T
+VW = C // 2
+EPS = 1e-5
+NEG = -1.0e9
+SCALE = 1.0 / math.sqrt(DH)
+
+FLOPS = 4 * 2 * C * C * N + 2 * 2 * B * H * DH * (T * (T + 1) // 2)
+
+
+def tile_microgpttorch_b_kernel(tc, embedding, pos, gamma, beta, wq, wk, wv, wo, offs, out):
+    nc = tc.nc
+    with (
+        tc.tile_pool(name="held", bufs=1) as held,
+        tc.tile_pool(name="norm", bufs=2) as norm,
+    ):
+        offsets = held.tile([P, N // 16], U16, name="offsets")
+        nc.sync.dma_start(offsets[:], offs)
+        pos_sb = held.tile([P, CB, T], F32, name="pos_sb")
+        nc.sync.dma_start(pos_sb[:], pos.rearrange("(b p) t -> p b t", p=P))
+        gamma_sb = held.tile([P, CB], F32, name="gamma_sb")
+        beta_sb = held.tile([P, CB], F32, name="beta_sb")
+        with nc.allow_non_contiguous_dma(reason="768 values, one to a partition in each of 6 columns"):
+            nc.scalar.dma_start(gamma_sb[:], gamma.rearrange("(b p) o -> p (b o)", p=P))
+            nc.scalar.dma_start(beta_sb[:], beta.rearrange("(b p) o -> p (b o)", p=P))
+
+        ident = held.tile([P, P], BF16, name="ident")
+        make_identity(nc, ident[:])
+        mean_w = held.tile([P, P], F32, name="mean_w")
+        nc.vector.memset(mean_w[:], 1.0 / C)
+        mask = held.tile([P, T], F32, name="mask")
+        nc.gpsimd.memset(mask[:], 0.0)
+        nc.gpsimd.affine_select(
+            out=mask[:, P:T], in_=mask[:, P:T], pattern=[[-1, P]], compare_op=ALU.is_ge,
+            fill=NEG, base=0, channel_multiplier=1,
+        )
+        warm = held.tile([P, 1], F32, name="warm")
+        nc.scalar.activation(warm[:], mean_w[:, 0:1], ACT.Ln)
+
+        x = [held.tile([P, N], F32, name=f"x{b}") for b in range(CB)]
+        h = [[held.tile([P, HALF], BF16, name=f"h{f}_{b}") for b in range(CB)] for f in range(2)]
+        mean = [held.tile([P, HALF], F32, name=f"mean{f}") for f in range(2)]
+        rstd = [held.tile([P, HALF], F32, name=f"rstd{f}") for f in range(2)]
+        w_sb = {name: held.tile([P, CB, C], BF16, name=f"w{name}_sb") for name in ("q", "k", "v", "o")}
+
+        with (
+            tc.tile_pool(name="table", bufs=1) as table,
+            tc.psum_pool(name="stats", bufs=1) as stats,
+        ):
+            emb = [table.tile([P, V], F32, name=f"emb{b}") for b in range(CB)]
+            for b in range(CB):
+                nc.sync.dma_start(emb[b][:], embedding[b * P : (b + 1) * P, :])
+
+            for name, w in (("v", wv), ("q", wq), ("k", wk), ("o", wo)):
+                nc.sync.dma_start(w_sb[name][:], w.rearrange("(b p) m -> p b m", p=P))
+
+            mean_ps = [stats.tile([P, HALF], F32, name=f"mean_ps{f}") for f in range(2)]
+            sq_ps = [stats.tile([P, HALF], F32, name=f"sq_ps{f}") for f in range(2)]
+            for b in range(CB):
+                for s in range(B):
+                    nc.vector.tensor_tensor(
+                        x[b][:, s * T : (s + 1) * T],
+                        emb[b][:].indirect(offsets[:, s * (T // 16) : (s + 1) * (T // 16)]),
+                        pos_sb[:, b, :],
+                        ALU.add,
+                    )
+                for f in range(2):
+                    cols = slice(f * HALF, (f + 1) * HALF)
+                    xx = norm.tile([P, HALF], F32, name="xx")
+                    nc.scalar.activation(xx[:], x[b][:, cols], ACT.Square)
+                    nc.tensor.matmul(mean_ps[f][:], mean_w[:], x[b][:, cols], start=(b == 0), stop=(b == CB - 1))
+                    nc.tensor.matmul(sq_ps[f][:], mean_w[:], xx[:], start=(b == 0), stop=(b == CB - 1))
+
+            logs = []
+            for f in range(2):
+                nc.scalar.copy(mean[f][:], mean_ps[f][:])
+                mm = norm.tile([P, HALF], F32, name="mm")
+                nc.scalar.activation(mm[:], mean_ps[f][:], ACT.Square)
+                var = norm.tile([P, HALF], F32, name="var")
+                nc.vector.tensor_tensor(var[:], sq_ps[f][:], mm[:], ALU.subtract)
+                nc.vector.tensor_scalar(var[:], var[:], 0.0, EPS, ALU.max, ALU.add)
+                nc.scalar.activation(var[:], var[:], ACT.Ln)
+                logs.append(var)
+            for f in range(2):
+                nc.scalar.activation(rstd[f][:], logs[f][:], ACT.Exp, scale=-0.5)
+
+        for f in range(2):
+            cols = slice(f * HALF, (f + 1) * HALF)
+            for b in range(CB):
+                cen = norm.tile([P, HALF], F32, name="cen")
+                nc.vector.tensor_tensor(cen[:], x[b][:, cols], mean[f][:], ALU.subtract)
+                nc.vector.tensor_tensor(cen[:], cen[:], rstd[f][:], ALU.mult)
+                nc.scalar.activation(
+                    h[f][b][:], cen[:], ACT.Identity, bias=beta_sb[:, b : b + 1], scale=gamma_sb[:, b : b + 1]
+                )
+
+        with (
+            tc.tile_pool(name="kept", bufs=1) as kept,
+            tc.tile_pool(name="heads", bufs=3) as heads,
+            tc.tile_pool(name="result", bufs=3) as result,
+            tc.psum_pool(name="psum", bufs=1) as psum,
+        ):
+            for f in range(2):
+                cols = slice(f * HALF, (f + 1) * HALF)
+
+                v_t = []
+                for tb in range(HALF // P):
+                    v_t.append(kept.tile([P, C], BF16, name=f"v_t{f}_{tb}"))
+                    for part in range(C // VW):
+                        acc = psum.tile([P, HALF], F32, name="acc", bufs=2)
+                        for b in range(CB):
+                            nc.tensor.matmul(
+                                acc[:, :VW],
+                                h[f][b][:, tb * P : (tb + 1) * P],
+                                w_sb["v"][:, b, part * VW : (part + 1) * VW],
+                                start=(b == 0),
+                                stop=(b == CB - 1),
+                            )
+                        nc.scalar.copy(v_t[tb][:, part * VW : (part + 1) * VW], acc[:, :VW])
+
+                attn = []
+                for a in range(H):
+                    rows = slice(a * DH, (a + 1) * DH)
+
+                    qk = {}
+                    for name in ("q", "k"):
+                        acc = psum.tile([P, HALF], F32, name="acc", bufs=2)
+                        for b in range(CB):
+                            nc.tensor.matmul(
+                                acc[:], w_sb[name][:, b, rows], h[f][b][:], start=(b == 0), stop=(b == CB - 1)
+                            )
+                        qk[name] = heads.tile([P, HALF], BF16, name=name)
+                        nc.scalar.copy(qk[name][:], acc[:])
+                    q, k = qk["q"], qk["k"]
+
+                    sc_lo = psum.tile([P, SEQS, P], F32, name="sc_lo")
+                    sc_hi = psum.tile([P, SEQS, T], F32, name="sc_hi", bufs=2)
+                    for s in range(SEQS):
+                        t0 = s * T
+                        nc.tensor.matmul(sc_lo[:, s, :], q[:, t0 : t0 + P], k[:, t0 : t0 + P], start=True, stop=True)
+                        nc.tensor.matmul(sc_hi[:, s, :], q[:, t0 + P : t0 + T], k[:, t0 : t0 + T], start=True, stop=True)
+
+                    e_lo = heads.tile([P, SEQS, P], F32, name="e_lo")
+                    e_hi = heads.tile([P, SEQS, T], F32, name="e_hi")
+                    nc.vector.scalar_tensor_tensor(
+                        e_lo[:], sc_lo[:], SCALE, mask[:, P:T].unsqueeze(1).to_broadcast([P, SEQS, P]), ALU.mult, ALU.add
+                    )
+                    nc.vector.scalar_tensor_tensor(
+                        e_hi[:], sc_hi[:], SCALE, mask[:].unsqueeze(1).to_broadcast([P, SEQS, T]), ALU.mult, ALU.add
+                    )
+                    neg_max = heads.tile([P, 2 * SEQS], F32, name="neg_max")
+                    nc.vector.tensor_reduce(neg_max[:, :SEQS], e_lo[:], AXIS.X, ALU.max, negate=True)
+                    nc.vector.tensor_reduce(neg_max[:, SEQS:], e_hi[:], AXIS.X, ALU.max, negate=True)
+                    total = heads.tile([P, 2 * SEQS], F32, name="total")
+                    for s in range(SEQS):
+                        nc.scalar.activation(
+                            e_lo[:, s, :], e_lo[:, s, :], ACT.Exp,
+                            bias=neg_max[:, s : s + 1], accum_out=total[:, s : s + 1],
+                        )
+                        nc.scalar.activation(
+                            e_hi[:, s, :], e_hi[:, s, :], ACT.Exp,
+                            bias=neg_max[:, SEQS + s : SEQS + s + 1], accum_out=total[:, SEQS + s : SEQS + s + 1],
+                        )
+                    inv = heads.tile([P, 2 * SEQS], F32, name="inv")
+                    nc.vector.reciprocal(inv[:], total[:])
+                    p_lo = heads.tile([P, SEQS, P], BF16, name="p_lo")
+                    p_hi = heads.tile([P, SEQS, T], BF16, name="p_hi")
+                    for s in range(SEQS):
+                        nc.vector.tensor_scalar(p_lo[:, s, :], e_lo[:, s, :], inv[:, s : s + 1], None, ALU.mult)
+                        nc.vector.tensor_scalar(p_hi[:, s, :], e_hi[:, s, :], inv[:, SEQS + s : SEQS + s + 1], None, ALU.mult)
+
+                    p_t_ps = psum.tile([P, SEQS, T + P], BF16, name="p_t_ps")
+                    for s in range(SEQS):
+                        nc.tensor.transpose(p_t_ps[:, s, 0:P], p_lo[:, s, :], ident[:])
+                        nc.tensor.transpose(p_t_ps[:, s, P:T], p_hi[:, s, 0:P], ident[:])
+                        nc.tensor.transpose(p_t_ps[:, s, T : T + P], p_hi[:, s, P:T], ident[:])
+                    p_t = heads.tile([P, SEQS, T + P], BF16, name="p_t")
+                    nc.vector.tensor_copy(p_t[:], p_t_ps[:])
+
+                    at_ps = psum.tile([P, HALF], F32, name="at_ps", bufs=2)
+                    for s in range(SEQS):
+                        t0 = s * T
+                        nc.tensor.matmul(
+                            at_ps[:, t0 : t0 + T], v_t[2 * s][:, rows], p_t[:, s, 0:T], start=True, stop=False
+                        )
+                        nc.tensor.matmul(
+                            at_ps[:, t0 + P : t0 + T], v_t[2 * s + 1][:, rows], p_t[:, s, T : T + P], start=False, stop=True
+                        )
+                    attn.append(kept.tile([P, HALF], BF16, name=f"attn{f}_{a}"))
+                    nc.scalar.copy(attn[a][:], at_ps[:])
+
+                for b in range(CB):
+                    acc = psum.tile([P, HALF], F32, name="acc", bufs=2)
+                    for a in range(H):
+                        nc.tensor.matmul(
+                            acc[:], w_sb["o"][:, a, b * P : (b + 1) * P], attn[a][:], start=(a == 0), stop=(a == H - 1)
+                        )
+                    y = result.tile([P, HALF], F32, name="y")
+                    nc.vector.tensor_tensor(y[:], acc[:], x[b][:, cols], ALU.add)
+                    nc.sync.dma_start(out[b * P : (b + 1) * P, cols], y[:])

@@ -19,6 +19,8 @@ VW = C // 2
 EPS = 1e-5
 NEG = -1.0e9
 SCALE = 1.0 / math.sqrt(DH)
+LAG = 3
+assert 2 * LAG == CB
 
 FLOPS = 4 * 2 * C * C * N + 2 * 2 * B * H * DH * (T * (T + 1) // 2)
 
@@ -115,12 +117,11 @@ def tile_microgpttorch_b_kernel(tc, embedding, pos, gamma, beta, wq, wk, wv, wo,
             tc.tile_pool(name="result", bufs=3) as result,
             tc.psum_pool(name="psum", bufs=1) as psum,
         ):
-            for f in range(2):
-                cols = slice(f * HALF, (f + 1) * HALF)
+            v_t = [[kept.tile([P, C], BF16, name=f"v_t{f}_{tb}") for tb in range(HALF // P)] for f in range(2)]
+            attn = [[kept.tile([P, HALF], BF16, name=f"attn{f}_{a}") for a in range(H)] for f in range(2)]
 
-                v_t = []
+            def project_v(f):
                 for tb in range(HALF // P):
-                    v_t.append(kept.tile([P, C], BF16, name=f"v_t{f}_{tb}"))
                     for part in range(C // VW):
                         acc = psum.tile([P, HALF], F32, name="acc", bufs=2)
                         for b in range(CB):
@@ -131,85 +132,108 @@ def tile_microgpttorch_b_kernel(tc, embedding, pos, gamma, beta, wq, wk, wv, wo,
                                 start=(b == 0),
                                 stop=(b == CB - 1),
                             )
-                        nc.scalar.copy(v_t[tb][:, part * VW : (part + 1) * VW], acc[:, :VW])
+                        nc.scalar.copy(v_t[f][tb][:, part * VW : (part + 1) * VW], acc[:, :VW])
 
-                attn = []
-                for a in range(H):
-                    rows = slice(a * DH, (a + 1) * DH)
-
-                    qk = {}
-                    for name in ("q", "k"):
-                        acc = psum.tile([P, HALF], F32, name="acc", bufs=2)
-                        for b in range(CB):
-                            nc.tensor.matmul(
-                                acc[:], w_sb[name][:, b, rows], h[f][b][:], start=(b == 0), stop=(b == CB - 1)
-                            )
-                        qk[name] = heads.tile([P, HALF], BF16, name=name)
-                        nc.scalar.copy(qk[name][:], acc[:])
-                    q, k = qk["q"], qk["k"]
-
-                    sc_lo = psum.tile([P, SEQS, P], F32, name="sc_lo")
-                    sc_hi = psum.tile([P, SEQS, T], F32, name="sc_hi", bufs=2)
-                    for s in range(SEQS):
-                        t0 = s * T
-                        nc.tensor.matmul(sc_lo[:, s, :], q[:, t0 : t0 + P], k[:, t0 : t0 + P], start=True, stop=True)
-                        nc.tensor.matmul(sc_hi[:, s, :], q[:, t0 + P : t0 + T], k[:, t0 : t0 + T], start=True, stop=True)
-
-                    e_lo = heads.tile([P, SEQS, P], F32, name="e_lo")
-                    e_hi = heads.tile([P, SEQS, T], F32, name="e_hi")
-                    nc.vector.scalar_tensor_tensor(
-                        e_lo[:], sc_lo[:], SCALE, mask[:, P:T].unsqueeze(1).to_broadcast([P, SEQS, P]), ALU.mult, ALU.add
-                    )
-                    nc.vector.scalar_tensor_tensor(
-                        e_hi[:], sc_hi[:], SCALE, mask[:].unsqueeze(1).to_broadcast([P, SEQS, T]), ALU.mult, ALU.add
-                    )
-                    neg_max = heads.tile([P, 2 * SEQS], F32, name="neg_max")
-                    nc.vector.tensor_reduce(neg_max[:, :SEQS], e_lo[:], AXIS.X, ALU.max, negate=True)
-                    nc.vector.tensor_reduce(neg_max[:, SEQS:], e_hi[:], AXIS.X, ALU.max, negate=True)
-                    total = heads.tile([P, 2 * SEQS], F32, name="total")
-                    for s in range(SEQS):
-                        nc.scalar.activation(
-                            e_lo[:, s, :], e_lo[:, s, :], ACT.Exp,
-                            bias=neg_max[:, s : s + 1], accum_out=total[:, s : s + 1],
-                        )
-                        nc.scalar.activation(
-                            e_hi[:, s, :], e_hi[:, s, :], ACT.Exp,
-                            bias=neg_max[:, SEQS + s : SEQS + s + 1], accum_out=total[:, SEQS + s : SEQS + s + 1],
-                        )
-                    inv = heads.tile([P, 2 * SEQS], F32, name="inv")
-                    nc.vector.reciprocal(inv[:], total[:])
-                    p_lo = heads.tile([P, SEQS, P], BF16, name="p_lo")
-                    p_hi = heads.tile([P, SEQS, T], BF16, name="p_hi")
-                    for s in range(SEQS):
-                        nc.vector.tensor_scalar(p_lo[:, s, :], e_lo[:, s, :], inv[:, s : s + 1], None, ALU.mult)
-                        nc.vector.tensor_scalar(p_hi[:, s, :], e_hi[:, s, :], inv[:, SEQS + s : SEQS + s + 1], None, ALU.mult)
-
-                    p_t_ps = psum.tile([P, SEQS, T + P], BF16, name="p_t_ps")
-                    for s in range(SEQS):
-                        nc.tensor.transpose(p_t_ps[:, s, 0:P], p_lo[:, s, :], ident[:])
-                        nc.tensor.transpose(p_t_ps[:, s, P:T], p_hi[:, s, 0:P], ident[:])
-                        nc.tensor.transpose(p_t_ps[:, s, T : T + P], p_hi[:, s, P:T], ident[:])
-                    p_t = heads.tile([P, SEQS, T + P], BF16, name="p_t")
-                    nc.vector.tensor_copy(p_t[:], p_t_ps[:])
-
-                    at_ps = psum.tile([P, HALF], F32, name="at_ps", bufs=2)
-                    for s in range(SEQS):
-                        t0 = s * T
-                        nc.tensor.matmul(
-                            at_ps[:, t0 : t0 + T], v_t[2 * s][:, rows], p_t[:, s, 0:T], start=True, stop=False
-                        )
-                        nc.tensor.matmul(
-                            at_ps[:, t0 + P : t0 + T], v_t[2 * s + 1][:, rows], p_t[:, s, T : T + P], start=False, stop=True
-                        )
-                    attn.append(kept.tile([P, HALF], BF16, name=f"attn{f}_{a}"))
-                    nc.scalar.copy(attn[a][:], at_ps[:])
-
+            def project_head(name, f, a):
+                acc = psum.tile([P, HALF], F32, name="acc", bufs=2)
                 for b in range(CB):
-                    acc = psum.tile([P, HALF], F32, name="acc", bufs=2)
-                    for a in range(H):
-                        nc.tensor.matmul(
-                            acc[:], w_sb["o"][:, a, b * P : (b + 1) * P], attn[a][:], start=(a == 0), stop=(a == H - 1)
-                        )
-                    y = result.tile([P, HALF], F32, name="y")
-                    nc.vector.tensor_tensor(y[:], acc[:], x[b][:, cols], ALU.add)
-                    nc.sync.dma_start(out[b * P : (b + 1) * P, cols], y[:])
+                    nc.tensor.matmul(
+                        acc[:], w_sb[name][:, b, a * DH : (a + 1) * DH], h[f][b][:], start=(b == 0), stop=(b == CB - 1)
+                    )
+                rounded = heads.tile([P, HALF], BF16, name=name)
+                nc.scalar.copy(rounded[:], acc[:])
+                return rounded
+
+            def softmax_weights(q, k):
+                sc_lo = psum.tile([P, SEQS, P], F32, name="sc_lo")
+                sc_hi = psum.tile([P, SEQS, T], F32, name="sc_hi", bufs=2)
+                for s in range(SEQS):
+                    t0 = s * T
+                    nc.tensor.matmul(sc_lo[:, s, :], q[:, t0 : t0 + P], k[:, t0 : t0 + P], start=True, stop=True)
+                    nc.tensor.matmul(sc_hi[:, s, :], q[:, t0 + P : t0 + T], k[:, t0 : t0 + T], start=True, stop=True)
+                e_lo = heads.tile([P, SEQS, P], F32, name="e_lo")
+                e_hi = heads.tile([P, SEQS, T], F32, name="e_hi")
+                nc.vector.scalar_tensor_tensor(
+                    e_lo[:], sc_lo[:], SCALE, mask[:, P:T].unsqueeze(1).to_broadcast([P, SEQS, P]), ALU.mult, ALU.add
+                )
+                nc.vector.scalar_tensor_tensor(
+                    e_hi[:], sc_hi[:], SCALE, mask[:].unsqueeze(1).to_broadcast([P, SEQS, T]), ALU.mult, ALU.add
+                )
+                neg_max = heads.tile([P, 2 * SEQS], F32, name="neg_max")
+                nc.vector.tensor_reduce(neg_max[:, :SEQS], e_lo[:], AXIS.X, ALU.max, negate=True)
+                nc.vector.tensor_reduce(neg_max[:, SEQS:], e_hi[:], AXIS.X, ALU.max, negate=True)
+                total = heads.tile([P, 2 * SEQS], F32, name="total")
+                for s in range(SEQS):
+                    nc.scalar.activation(
+                        e_lo[:, s, :], e_lo[:, s, :], ACT.Exp,
+                        bias=neg_max[:, s : s + 1], accum_out=total[:, s : s + 1],
+                    )
+                    nc.scalar.activation(
+                        e_hi[:, s, :], e_hi[:, s, :], ACT.Exp,
+                        bias=neg_max[:, SEQS + s : SEQS + s + 1], accum_out=total[:, SEQS + s : SEQS + s + 1],
+                    )
+                inv = heads.tile([P, 2 * SEQS], F32, name="inv")
+                nc.vector.reciprocal(inv[:], total[:])
+                p_lo = heads.tile([P, SEQS, P], BF16, name="p_lo")
+                p_hi = heads.tile([P, SEQS, T], BF16, name="p_hi")
+                for s in range(SEQS):
+                    nc.vector.tensor_scalar(p_lo[:, s, :], e_lo[:, s, :], inv[:, s : s + 1], None, ALU.mult)
+                    nc.vector.tensor_scalar(p_hi[:, s, :], e_hi[:, s, :], inv[:, SEQS + s : SEQS + s + 1], None, ALU.mult)
+                return p_lo, p_hi
+
+            def transpose_weights(p_lo, p_hi):
+                p_t_ps = psum.tile([P, SEQS, T + P], BF16, name="p_t_ps")
+                for s in range(SEQS):
+                    nc.tensor.transpose(p_t_ps[:, s, 0:P], p_lo[:, s, :], ident[:])
+                    nc.tensor.transpose(p_t_ps[:, s, P:T], p_hi[:, s, 0:P], ident[:])
+                    nc.tensor.transpose(p_t_ps[:, s, T : T + P], p_hi[:, s, P:T], ident[:])
+                p_t = heads.tile([P, SEQS, T + P], BF16, name="p_t")
+                nc.vector.tensor_copy(p_t[:], p_t_ps[:])
+                return p_t
+
+            def attend(f, a, p_t):
+                rows = slice(a * DH, (a + 1) * DH)
+                at_ps = psum.tile([P, HALF], F32, name="at_ps", bufs=2)
+                for s in range(SEQS):
+                    t0 = s * T
+                    nc.tensor.matmul(
+                        at_ps[:, t0 : t0 + T], v_t[f][2 * s][:, rows], p_t[:, s, 0:T], start=True, stop=False
+                    )
+                    nc.tensor.matmul(
+                        at_ps[:, t0 + P : t0 + T], v_t[f][2 * s + 1][:, rows], p_t[:, s, T : T + P], start=False, stop=True
+                    )
+                nc.scalar.copy(attn[f][a][:], at_ps[:])
+
+            def output_block(f, b):
+                cols = slice(f * HALF, (f + 1) * HALF)
+                acc = psum.tile([P, HALF], F32, name="acc", bufs=2)
+                for a in range(H):
+                    nc.tensor.matmul(
+                        acc[:], w_sb["o"][:, a, b * P : (b + 1) * P], attn[f][a][:], start=(a == 0), stop=(a == H - 1)
+                    )
+                y = result.tile([P, HALF], F32, name="y")
+                nc.vector.tensor_tensor(y[:], acc[:], x[b][:, cols], ALU.add)
+                nc.sync.dma_start(out[b * P : (b + 1) * P, cols], y[:])
+
+            steps = [(f, a) for f in range(2) for a in range(H)]
+            q, k, p, p_t = {}, {}, {}, {}
+            project_v(0)
+            for i in range(len(steps) + LAG):
+                if i == H:
+                    project_v(1)
+                if i < len(steps):
+                    q[i] = project_head("q", *steps[i])
+                else:
+                    output_block(0, 2 * (i - len(steps)))
+                if i >= LAG:
+                    attend(*steps[i - LAG], p_t[i - LAG])
+                if 1 <= i <= len(steps):
+                    p[i - 1] = softmax_weights(q[i - 1], k[i - 1])
+                if i < len(steps):
+                    k[i] = project_head("k", *steps[i])
+                else:
+                    output_block(0, 2 * (i - len(steps)) + 1)
+                if 2 <= i <= len(steps) + 1:
+                    p_t[i - 2] = transpose_weights(*p[i - 2])
+            for b in range(CB):
+                output_block(1, b)

@@ -29,7 +29,8 @@ def tile_microgpttorch_b_kernel(tc, embedding, pos, gamma, beta, wq, wk, wv, wo,
     nc = tc.nc
     with (
         tc.tile_pool(name="held", bufs=1) as held,
-        tc.tile_pool(name="norm", bufs=2) as norm,
+        tc.tile_pool(name="norm", bufs=3) as norm,
+        tc.psum_pool(name="psum", bufs=4) as psum,
     ):
         offsets = held.tile([P, N // 16], U16, name="offsets")
         nc.sync.dma_start(offsets[:], offs)
@@ -52,90 +53,77 @@ def tile_microgpttorch_b_kernel(tc, embedding, pos, gamma, beta, wq, wk, wv, wo,
             fill=NEG, base=0, channel_multiplier=1,
         )
         warm = held.tile([P, 1], F32, name="warm")
-        nc.scalar.activation(warm[:], mean_w[:, 0:1], ACT.Ln)
+        nc.scalar.activation(warm[:], mean_w[:, 0:1], ACT.Abs_reciprocal_sqrt)
 
-        x = [held.tile([P, N], F32, name=f"x{b}") for b in range(CB)]
+        xs = [held.tile([P, B, 2 * T], F32, name=f"xs{b}") for b in range(CB)]
         h = [[held.tile([P, HALF], BF16, name=f"h{f}_{b}") for b in range(CB)] for f in range(2)]
-        mean = [held.tile([P, HALF], F32, name=f"mean{f}") for f in range(2)]
-        rstd = [held.tile([P, HALF], F32, name=f"rstd{f}") for f in range(2)]
+        mean = held.tile([P, B, T], F32, name="mean")
+        rstd = held.tile([P, B, T], F32, name="rstd")
         w_sb = {name: held.tile([P, CB, C], BF16, name=f"w{name}_sb") for name in ("q", "k", "v", "o")}
 
-        with (
-            tc.tile_pool(name="table", bufs=1) as table,
-            tc.psum_pool(name="stats", bufs=1) as stats,
-        ):
+        moments = [psum.tile([P, 2 * T], F32, name=f"moments{s}", tag="short") for s in range(B)]
+        with tc.tile_pool(name="table", bufs=1) as table:
             emb = [table.tile([P, V], F32, name=f"emb{b}") for b in range(CB)]
             for b in range(CB):
                 nc.sync.dma_start(emb[b][:], embedding[b * P : (b + 1) * P, :])
-
             for name, w in (("v", wv), ("q", wq), ("k", wk), ("o", wo)):
                 nc.sync.dma_start(w_sb[name][:], w.rearrange("(b p) m -> p b m", p=P))
-
-            mean_ps = [stats.tile([P, HALF], F32, name=f"mean_ps{f}") for f in range(2)]
-            sq_ps = [stats.tile([P, HALF], F32, name=f"sq_ps{f}") for f in range(2)]
             for b in range(CB):
                 for s in range(B):
                     nc.vector.tensor_tensor(
-                        x[b][:, s * T : (s + 1) * T],
+                        xs[b][:, s, 0:T],
                         emb[b][:].indirect(offsets[:, s * (T // 16) : (s + 1) * (T // 16)]),
                         pos_sb[:, b, :],
                         ALU.add,
                     )
-                for f in range(2):
-                    cols = slice(f * HALF, (f + 1) * HALF)
-                    xx = norm.tile([P, HALF], F32, name="xx")
-                    nc.scalar.activation(xx[:], x[b][:, cols], ACT.Square)
-                    nc.tensor.matmul(mean_ps[f][:], mean_w[:], x[b][:, cols], start=(b == 0), stop=(b == CB - 1))
-                    nc.tensor.matmul(sq_ps[f][:], mean_w[:], xx[:], start=(b == 0), stop=(b == CB - 1))
+                    nc.scalar.activation(xs[b][:, s, T : 2 * T], xs[b][:, s, 0:T], ACT.Square)
+                    nc.tensor.matmul(moments[s][:], mean_w[:], xs[b][:, s, :], start=(b == 0), stop=(b == CB - 1))
 
-            logs = []
-            for f in range(2):
-                nc.scalar.copy(mean[f][:], mean_ps[f][:])
-                mm = norm.tile([P, HALF], F32, name="mm")
-                nc.scalar.activation(mm[:], mean_ps[f][:], ACT.Square)
-                var = norm.tile([P, HALF], F32, name="var")
-                nc.vector.tensor_tensor(var[:], sq_ps[f][:], mm[:], ALU.subtract)
-                nc.vector.tensor_scalar(var[:], var[:], 0.0, EPS, ALU.max, ALU.add)
-                nc.scalar.activation(var[:], var[:], ACT.Ln)
-                logs.append(var)
-            for f in range(2):
-                nc.scalar.activation(rstd[f][:], logs[f][:], ACT.Exp, scale=-0.5)
+        def statistics(s):
+            mm = norm.tile([P, T], F32, name="mm")
+            nc.scalar.activation(mm[:], moments[s][:, 0:T], ACT.Square)
+            nc.scalar.copy(mean[:, s, :], moments[s][:, 0:T])
+            var = norm.tile([P, T], F32, name="var")
+            nc.vector.tensor_tensor(var[:], moments[s][:, T : 2 * T], mm[:], ALU.subtract)
+            nc.vector.tensor_scalar(var[:], var[:], 0.0, EPS, ALU.max, ALU.add)
+            nc.scalar.activation(rstd[:, s, :], var[:], ACT.Abs_reciprocal_sqrt)
 
-        for f in range(2):
-            cols = slice(f * HALF, (f + 1) * HALF)
-            for b in range(CB):
-                cen = norm.tile([P, HALF], F32, name="cen")
-                nc.vector.tensor_tensor(cen[:], x[b][:, cols], mean[f][:], ALU.subtract)
-                nc.vector.tensor_tensor(cen[:], cen[:], rstd[f][:], ALU.mult)
-                nc.scalar.activation(
-                    h[f][b][:], cen[:], ACT.Identity, bias=beta_sb[:, b : b + 1], scale=gamma_sb[:, b : b + 1]
-                )
+        def normalise(b, s):
+            cen = norm.tile([P, T], F32, name="cen")
+            nc.vector.tensor_tensor(cen[:], xs[b][:, s, 0:T], mean[:, s, :], ALU.subtract)
+            nc.vector.tensor_tensor(cen[:], cen[:], rstd[:, s, :], ALU.mult)
+            nc.scalar.activation(
+                h[s // SEQS][b][:, (s % SEQS) * T : (s % SEQS + 1) * T], cen[:], ACT.Identity,
+                bias=beta_sb[:, b : b + 1], scale=gamma_sb[:, b : b + 1],
+            )
 
         with (
             tc.tile_pool(name="kept", bufs=1) as kept,
             tc.tile_pool(name="heads", bufs=3) as heads,
             tc.tile_pool(name="result", bufs=3) as result,
-            tc.psum_pool(name="psum", bufs=1) as psum,
         ):
             v_t = [[kept.tile([P, C], BF16, name=f"v_t{f}_{tb}") for tb in range(HALF // P)] for f in range(2)]
             attn = [[kept.tile([P, HALF], BF16, name=f"attn{f}_{a}") for a in range(H)] for f in range(2)]
 
-            def project_v(f):
-                for tb in range(HALF // P):
-                    for part in range(C // VW):
-                        acc = psum.tile([P, HALF], F32, name="acc", bufs=2)
-                        for b in range(CB):
+            def project_v(f, s):
+                sums = [psum.tile([P, HALF], F32, name=f"v_sum{j}", tag="acc") for j in range(4)]
+                for b in range(CB):
+                    for tb in range(T // P):
+                        for part in range(C // VW):
                             nc.tensor.matmul(
-                                acc[:, :VW],
-                                h[f][b][:, tb * P : (tb + 1) * P],
+                                sums[2 * tb + part][:, :VW],
+                                h[f][b][:, s * T + tb * P : s * T + (tb + 1) * P],
                                 w_sb["v"][:, b, part * VW : (part + 1) * VW],
                                 start=(b == 0),
                                 stop=(b == CB - 1),
                             )
-                        nc.scalar.copy(v_t[f][tb][:, part * VW : (part + 1) * VW], acc[:, :VW])
+                for tb in range(T // P):
+                    rounded = v_t[f][2 * s + tb]
+                    nc.scalar.copy(rounded[:, :VW], sums[2 * tb][:, :VW])
+                    nc.vector.tensor_copy(rounded[:, VW:], sums[2 * tb + 1][:, :VW])
 
             def project_head(name, f, a):
-                acc = psum.tile([P, HALF], F32, name="acc", bufs=2)
+                acc = psum.tile([P, HALF], F32, name="acc")
                 for b in range(CB):
                     nc.tensor.matmul(
                         acc[:], w_sb[name][:, b, a * DH : (a + 1) * DH], h[f][b][:], start=(b == 0), stop=(b == CB - 1)
@@ -145,8 +133,8 @@ def tile_microgpttorch_b_kernel(tc, embedding, pos, gamma, beta, wq, wk, wv, wo,
                 return rounded
 
             def softmax_weights(q, k):
-                sc_lo = psum.tile([P, SEQS, P], F32, name="sc_lo")
-                sc_hi = psum.tile([P, SEQS, T], F32, name="sc_hi", bufs=2)
+                sc_lo = psum.tile([P, SEQS, P], F32, name="sc_lo", tag="short")
+                sc_hi = psum.tile([P, SEQS, T], F32, name="sc_hi", tag="short")
                 for s in range(SEQS):
                     t0 = s * T
                     nc.tensor.matmul(sc_lo[:, s, :], q[:, t0 : t0 + P], k[:, t0 : t0 + P], start=True, stop=True)
@@ -182,18 +170,18 @@ def tile_microgpttorch_b_kernel(tc, embedding, pos, gamma, beta, wq, wk, wv, wo,
                 return p_lo, p_hi
 
             def transpose_weights(p_lo, p_hi):
-                p_t_ps = psum.tile([P, SEQS, T + P], BF16, name="p_t_ps")
+                p_t_ps = psum.tile([P, SEQS, T + P], BF16, name="p_t_ps", tag="short")
                 for s in range(SEQS):
                     nc.tensor.transpose(p_t_ps[:, s, 0:P], p_lo[:, s, :], ident[:])
                     nc.tensor.transpose(p_t_ps[:, s, P:T], p_hi[:, s, 0:P], ident[:])
                     nc.tensor.transpose(p_t_ps[:, s, T : T + P], p_hi[:, s, P:T], ident[:])
                 p_t = heads.tile([P, SEQS, T + P], BF16, name="p_t")
-                nc.vector.tensor_copy(p_t[:], p_t_ps[:])
+                nc.scalar.copy(p_t[:], p_t_ps[:])
                 return p_t
 
             def attend(f, a, p_t):
                 rows = slice(a * DH, (a + 1) * DH)
-                at_ps = psum.tile([P, HALF], F32, name="at_ps", bufs=2)
+                at_ps = psum.tile([P, HALF], F32, name="at_ps", tag="short")
                 for s in range(SEQS):
                     t0 = s * T
                     nc.tensor.matmul(
@@ -205,22 +193,37 @@ def tile_microgpttorch_b_kernel(tc, embedding, pos, gamma, beta, wq, wk, wv, wo,
                 nc.scalar.copy(attn[f][a][:], at_ps[:])
 
             def output_block(f, b):
-                cols = slice(f * HALF, (f + 1) * HALF)
-                acc = psum.tile([P, HALF], F32, name="acc", bufs=2)
+                acc = psum.tile([P, HALF], F32, name="acc")
                 for a in range(H):
                     nc.tensor.matmul(
                         acc[:], w_sb["o"][:, a, b * P : (b + 1) * P], attn[f][a][:], start=(a == 0), stop=(a == H - 1)
                     )
                 y = result.tile([P, HALF], F32, name="y")
-                nc.vector.tensor_tensor(y[:], acc[:], x[b][:, cols], ALU.add)
-                nc.sync.dma_start(out[b * P : (b + 1) * P, cols], y[:])
+                nc.vector.tensor_tensor(
+                    y[:].rearrange("p (s t) -> p s t", s=SEQS),
+                    acc[:].rearrange("p (s t) -> p s t", s=SEQS),
+                    xs[b][:, f * SEQS : (f + 1) * SEQS, 0:T],
+                    ALU.add,
+                )
+                nc.sync.dma_start(out[b * P : (b + 1) * P, f * HALF : (f + 1) * HALF], y[:])
 
             steps = [(f, a) for f in range(2) for a in range(H)]
             q, k, p, p_t = {}, {}, {}, {}
-            project_v(0)
+            for s in range(SEQS):
+                statistics(s)
+            for s in range(SEQS):
+                for b in range(CB):
+                    normalise(b, s)
+                project_v(0, s)
+            for s in range(SEQS, B):
+                statistics(s)
             for i in range(len(steps) + LAG):
+                if i < CB:
+                    for s in range(SEQS, B):
+                        normalise(i, s)
                 if i == H:
-                    project_v(1)
+                    for s in range(SEQS):
+                        project_v(1, s)
                 if i < len(steps):
                     q[i] = project_head("q", *steps[i])
                 else:

@@ -88,13 +88,15 @@ def tile_microgpttorch_b_kernel(tc, embedding, pos, gamma, beta, wq, wk, wv, wo,
             nc.vector.tensor_scalar(var[:], var[:], 0.0, EPS, ALU.max, ALU.add)
             nc.scalar.activation(rstd[:, s, :], var[:], ACT.Abs_reciprocal_sqrt)
 
-        def normalise(b, s):
-            cen = norm.tile([P, T], F32, name="cen")
-            nc.vector.tensor_tensor(cen[:], xs[b][:, s, 0:T], mean[:, s, :], ALU.subtract)
-            nc.vector.tensor_tensor(cen[:], cen[:], rstd[:, s, :], ALU.mult)
+        def normalise(b, first, count):
+            seqs = slice(first, first + count)
+            start = (first % SEQS) * T
+            cen = norm.tile([P, count, T], F32, name="cen")
+            nc.vector.tensor_tensor(cen[:], xs[b][:, seqs, 0:T], mean[:, seqs, :], ALU.subtract)
+            nc.vector.tensor_tensor(cen[:], cen[:], rstd[:, seqs, :], ALU.mult)
             nc.scalar.activation(
-                h[s // SEQS][b][:, (s % SEQS) * T : (s % SEQS + 1) * T], cen[:], ACT.Identity,
-                bias=beta_sb[:, b : b + 1], scale=gamma_sb[:, b : b + 1],
+                h[first // SEQS][b][:, start : start + count * T].rearrange("p (s t) -> p s t", s=count),
+                cen[:], ACT.Identity, bias=beta_sb[:, b : b + 1], scale=gamma_sb[:, b : b + 1],
             )
 
         with (
@@ -176,7 +178,7 @@ def tile_microgpttorch_b_kernel(tc, embedding, pos, gamma, beta, wq, wk, wv, wo,
                     nc.tensor.transpose(p_t_ps[:, s, P:T], p_hi[:, s, 0:P], ident[:])
                     nc.tensor.transpose(p_t_ps[:, s, T : T + P], p_hi[:, s, P:T], ident[:])
                 p_t = heads.tile([P, SEQS, T + P], BF16, name="p_t")
-                nc.scalar.copy(p_t[:], p_t_ps[:])
+                nc.vector.tensor_copy(p_t[:], p_t_ps[:])
                 return p_t
 
             def attend(f, a, p_t):
@@ -213,14 +215,13 @@ def tile_microgpttorch_b_kernel(tc, embedding, pos, gamma, beta, wq, wk, wv, wo,
                 statistics(s)
             for s in range(SEQS):
                 for b in range(CB):
-                    normalise(b, s)
+                    normalise(b, s, 1)
                 project_v(0, s)
             for s in range(SEQS, B):
                 statistics(s)
             for i in range(len(steps) + LAG):
                 if i < CB:
-                    for s in range(SEQS, B):
-                        normalise(i, s)
+                    normalise(i, SEQS, SEQS)
                 if i == H:
                     for s in range(SEQS):
                         project_v(1, s)

@@ -108,21 +108,20 @@ def tile_microgpttorch_b_kernel(tc, embedding, pos, gamma, beta, wq, wk, wv, wo,
             attn = [[kept.tile([P, HALF], BF16, name=f"attn{f}_{a}") for a in range(H)] for f in range(2)]
 
             def project_v(f, s):
-                sums = [psum.tile([P, HALF], F32, name=f"v_sum{j}", tag="acc") for j in range(4)]
-                for b in range(CB):
-                    for tb in range(T // P):
+                for tb in range(T // P):
+                    sums = [psum.tile([P, HALF], F32, name=f"v_sum{part}", tag="acc") for part in range(C // VW)]
+                    for b in range(CB):
                         for part in range(C // VW):
                             nc.tensor.matmul(
-                                sums[2 * tb + part][:, :VW],
+                                sums[part][:, :VW],
                                 h[f][b][:, s * T + tb * P : s * T + (tb + 1) * P],
                                 w_sb["v"][:, b, part * VW : (part + 1) * VW],
                                 start=(b == 0),
                                 stop=(b == CB - 1),
                             )
-                for tb in range(T // P):
                     rounded = v_t[f][2 * s + tb]
-                    nc.scalar.copy(rounded[:, :VW], sums[2 * tb][:, :VW])
-                    nc.vector.tensor_copy(rounded[:, VW:], sums[2 * tb + 1][:, :VW])
+                    nc.scalar.copy(rounded[:, :VW], sums[0][:, :VW])
+                    nc.vector.tensor_copy(rounded[:, VW:], sums[1][:, :VW])
 
             def project_head(name, f, a):
                 acc = psum.tile([P, HALF], F32, name="acc")

@@ -35,7 +35,6 @@ def tile_microgpttorch_b_kernel(tc, embedding, pos, gamma, beta, wq, wk, wv, wo,
         offsets = held.tile([P, N // 16], U16, name="offsets")
         nc.sync.dma_start(offsets[:], offs)
         pos_sb = held.tile([P, CB, T], F32, name="pos_sb")
-        nc.sync.dma_start(pos_sb[:], pos.rearrange("(b p) t -> p b t", p=P))
         gamma_sb = held.tile([P, CB], F32, name="gamma_sb")
         beta_sb = held.tile([P, CB], F32, name="beta_sb")
         with nc.allow_non_contiguous_dma(reason="768 values, one to a partition in each of 6 columns"):
@@ -65,6 +64,7 @@ def tile_microgpttorch_b_kernel(tc, embedding, pos, gamma, beta, wq, wk, wv, wo,
         with tc.tile_pool(name="table", bufs=1) as table:
             emb = [table.tile([P, V], F32, name=f"emb{b}") for b in range(CB)]
             for b in range(CB):
+                nc.sync.dma_start(pos_sb[:, b, :], pos[b * P : (b + 1) * P, :])
                 nc.sync.dma_start(emb[b][:], embedding[b * P : (b + 1) * P, :])
             for name, w in (("v", wv), ("q", wq), ("k", wk), ("o", wo)):
                 nc.sync.dma_start(w_sb[name][:], w.rearrange("(b p) m -> p b m", p=P))
@@ -193,20 +193,26 @@ def tile_microgpttorch_b_kernel(tc, embedding, pos, gamma, beta, wq, wk, wv, wo,
                     )
                 nc.scalar.copy(attn[f][a][:], at_ps[:])
 
-            def output_block(f, b):
+            def output_block(f, b, first=0, count=SEQS):
+                width = count * T
                 acc = psum.tile([P, HALF], F32, name="acc")
                 for a in range(H):
                     nc.tensor.matmul(
-                        acc[:], w_sb["o"][:, a, b * P : (b + 1) * P], attn[f][a][:], start=(a == 0), stop=(a == H - 1)
+                        acc[:, :width],
+                        w_sb["o"][:, a, b * P : (b + 1) * P],
+                        attn[f][a][:, first * T : first * T + width],
+                        start=(a == 0),
+                        stop=(a == H - 1),
                     )
                 y = result.tile([P, HALF], F32, name="y")
                 nc.vector.tensor_tensor(
-                    y[:].rearrange("p (s t) -> p s t", s=SEQS),
-                    acc[:].rearrange("p (s t) -> p s t", s=SEQS),
-                    xs[b][:, f * SEQS : (f + 1) * SEQS, 0:T],
+                    y[:, :width].rearrange("p (s t) -> p s t", s=count),
+                    acc[:, :width].rearrange("p (s t) -> p s t", s=count),
+                    xs[b][:, f * SEQS + first : f * SEQS + first + count, 0:T],
                     ALU.add,
                 )
-                nc.sync.dma_start(out[b * P : (b + 1) * P, f * HALF : (f + 1) * HALF], y[:])
+                start = f * HALF + first * T
+                nc.sync.dma_start(out[b * P : (b + 1) * P, start : start + width], y[:, :width])
 
             steps = [(f, a) for f in range(2) for a in range(H)]
             q, k, p, p_t = {}, {}, {}, {}
@@ -238,5 +244,7 @@ def tile_microgpttorch_b_kernel(tc, embedding, pos, gamma, beta, wq, wk, wv, wo,
                     output_block(0, 2 * (i - len(steps)) + 1)
                 if 2 <= i <= len(steps) + 1:
                     p_t[i - 2] = transpose_weights(*p[i - 2])
-            for b in range(CB):
+            for b in range(CB - 1):
                 output_block(1, b)
+            for s in range(SEQS):
+                output_block(1, CB - 1, s, 1)

@@ -37,9 +37,6 @@ def tile_microgpttorch_b_kernel(tc, embedding, pos, gamma, beta, wq, wk, wv, wo,
         pos_sb = held.tile([P, CB, T], F32, name="pos_sb")
         gamma_sb = held.tile([P, CB], F32, name="gamma_sb")
         beta_sb = held.tile([P, CB], F32, name="beta_sb")
-        with nc.allow_non_contiguous_dma(reason="768 values, one to a partition in each of 6 columns"):
-            nc.scalar.dma_start(gamma_sb[:], gamma.rearrange("(b p) o -> p (b o)", p=P))
-            nc.scalar.dma_start(beta_sb[:], beta.rearrange("(b p) o -> p (b o)", p=P))
 
         ident = held.tile([P, P], BF16, name="ident")
         make_identity(nc, ident[:])
@@ -66,6 +63,9 @@ def tile_microgpttorch_b_kernel(tc, embedding, pos, gamma, beta, wq, wk, wv, wo,
             for b in range(CB):
                 nc.sync.dma_start(pos_sb[:, b, :], pos[b * P : (b + 1) * P, :])
                 nc.sync.dma_start(emb[b][:], embedding[b * P : (b + 1) * P, :])
+            with nc.allow_non_contiguous_dma(reason="768 values, one to a partition in each of 6 columns"):
+                nc.sync.dma_start(gamma_sb[:], gamma.rearrange("(b p) o -> p (b o)", p=P))
+                nc.sync.dma_start(beta_sb[:], beta.rearrange("(b p) o -> p (b o)", p=P))
             for name, w in (("v", wv), ("q", wq), ("k", wk), ("o", wo)):
                 nc.sync.dma_start(w_sb[name][:], w.rearrange("(b p) m -> p b m", p=P))
             for b in range(CB):

@@ -107,21 +107,19 @@ def tile_microgpttorch_b_kernel(tc, embedding, pos, gamma, beta, wq, wk, wv, wo,
             v_t = [[kept.tile([P, C], BF16, name=f"v_t{f}_{tb}") for tb in range(HALF // P)] for f in range(2)]
             attn = [[kept.tile([P, HALF], BF16, name=f"attn{f}_{a}") for a in range(H)] for f in range(2)]
 
-            def project_v(f, s):
-                for tb in range(T // P):
-                    sums = [psum.tile([P, HALF], F32, name=f"v_sum{part}", tag="acc") for part in range(C // VW)]
-                    for b in range(CB):
-                        for part in range(C // VW):
-                            nc.tensor.matmul(
-                                sums[part][:, :VW],
-                                h[f][b][:, s * T + tb * P : s * T + (tb + 1) * P],
-                                w_sb["v"][:, b, part * VW : (part + 1) * VW],
-                                start=(b == 0),
-                                stop=(b == CB - 1),
-                            )
-                    rounded = v_t[f][2 * s + tb]
-                    nc.scalar.copy(rounded[:, :VW], sums[0][:, :VW])
-                    nc.vector.tensor_copy(rounded[:, VW:], sums[1][:, :VW])
+            def project_v(f, tb):
+                sums = [psum.tile([P, HALF], F32, name=f"v_sum{part}", tag="acc") for part in range(C // VW)]
+                for b in range(CB):
+                    for part in range(C // VW):
+                        nc.tensor.matmul(
+                            sums[part][:, :VW],
+                            h[f][b][:, tb * P : (tb + 1) * P],
+                            w_sb["v"][:, b, part * VW : (part + 1) * VW],
+                            start=(b == 0),
+                            stop=(b == CB - 1),
+                        )
+                nc.scalar.copy(v_t[f][tb][:, :VW], sums[0][:, :VW])
+                nc.vector.tensor_copy(v_t[f][tb][:, VW:], sums[1][:, :VW])
 
             def project_head(name, f, a):
                 acc = psum.tile([P, HALF], F32, name="acc")
@@ -221,15 +219,14 @@ def tile_microgpttorch_b_kernel(tc, embedding, pos, gamma, beta, wq, wk, wv, wo,
             for s in range(SEQS):
                 for b in range(CB):
                     normalise(b, s, 1)
-                project_v(0, s)
+                if s == 0:
+                    project_v(0, 0)
+                    project_v(0, 1)
             for s in range(SEQS, B):
                 statistics(s)
             for i in range(len(steps) + LAG):
                 if i < CB:
                     normalise(i, SEQS, SEQS)
-                if i == H:
-                    for s in range(SEQS):
-                        project_v(1, s)
                 if i < len(steps):
                     q[i] = project_head("q", *steps[i])
                 else:
@@ -244,6 +241,10 @@ def tile_microgpttorch_b_kernel(tc, embedding, pos, gamma, beta, wq, wk, wv, wo,
                     output_block(0, 2 * (i - len(steps)) + 1)
                 if 2 <= i <= len(steps) + 1:
                     p_t[i - 2] = transpose_weights(*p[i - 2])
+                if i < 2:
+                    project_v(0, 2 + i)
+                if H - 1 <= i < H + LAG:
+                    project_v(1, i - (H - 1))
             for b in range(CB - 1):
                 output_block(1, b)
             for s in range(SEQS):

@@ -15,6 +15,9 @@ C, V, B, T, H, DH, N = 768, 4096, 4, 256, 6, 128, 1024
 CB = C // P
 HALF = 512
 SEQS = HALF // T
+ROWS = HALF // P
+UNITS = [(0, P), (P, P), (T, T)]
+SECOND = [(HALF, T), (HALF + T, T)]
 VW = C // 2
 EPS = 1e-5
 NEG = -1.0e9
@@ -40,6 +43,8 @@ def tile_microgpttorch_b_kernel(tc, embedding, pos, gamma, beta, wq, wk, wv, wo,
 
         ident = held.tile([P, P], BF16, name="ident")
         make_identity(nc, ident[:])
+        ident_f32 = held.tile([P, P], F32, name="ident_f32")
+        make_identity(nc, ident_f32[:])
         mean_w = held.tile([P, P], F32, name="mean_w")
         nc.vector.memset(mean_w[:], 1.0 / C)
         mask = held.tile([P, T], F32, name="mask")
@@ -51,13 +56,95 @@ def tile_microgpttorch_b_kernel(tc, embedding, pos, gamma, beta, wq, wk, wv, wo,
         warm = held.tile([P, 1], F32, name="warm")
         nc.scalar.activation(warm[:], mean_w[:, 0:1], ACT.Abs_reciprocal_sqrt)
 
-        xs = [held.tile([P, B, 2 * T], F32, name=f"xs{b}") for b in range(CB)]
+        xs = [held.tile([P, 2, N], F32, name=f"xs{b}") for b in range(CB)]
         h = [[held.tile([P, HALF], BF16, name=f"h{f}_{b}") for b in range(CB)] for f in range(2)]
-        mean = held.tile([P, B, T], F32, name="mean")
-        rstd = held.tile([P, B, T], F32, name="rstd")
+        row_sums = held.tile([P, 2, ROWS], F32, name="row_sums")
+        row_means = held.tile([P, 2, ROWS], F32, name="row_means")
+        squares = held.tile([P, P], F32, name="squares")
+        mean = held.tile([P, N], F32, name="mean")
+        rstd = held.tile([P, N], F32, name="rstd")
         w_sb = {name: held.tile([P, CB, C], BF16, name=f"w{name}_sb") for name in ("q", "k", "v", "o")}
+        v_t = [[held.tile([P, C], BF16, name=f"v_t{f}_{tb}") for tb in range(ROWS)] for f in range(2)]
 
-        moments = [psum.tile([P, 2 * T], F32, name=f"moments{s}", tag="short") for s in range(B)]
+        moments = {}
+        for tag, runs in (("acc", UNITS), ("short", SECOND)):
+            for start, count in runs:
+                moments[start] = psum.tile([P, 2, count], F32, name=f"moments{start}", tag=tag)
+
+        def look_up(b, start, count):
+            nc.vector.tensor_tensor(
+                xs[b][:, 0, start : start + count],
+                emb[b][:].indirect(offsets[:, start // 16 : (start + count) // 16]),
+                pos_sb[:, b, start % T : start % T + count],
+                ALU.add,
+            )
+
+        def add_moments(b, start, count):
+            entries = slice(start, start + count)
+            nc.scalar.activation(xs[b][:, 1, entries], xs[b][:, 0, entries], ACT.Square)
+            nc.tensor.matmul(
+                moments[start][:], mean_w[:], xs[b][:, :, entries], start=(b == 0), stop=(b == CB - 1)
+            )
+
+        def last_block_of_second_half():
+            for start, count in SECOND:
+                look_up(CB - 1, start, count)
+            x_rows = psum.tile([P, ROWS, P], F32, name="x_rows", tag="short")
+            for r in range(ROWS):
+                at = HALF + r * P
+                nc.tensor.transpose(x_rows[:, r, :], xs[CB - 1][:, 0, at : at + P], ident_f32[:])
+            nc.vector.tensor_reduce(row_sums[:, 0, :], x_rows[:], AXIS.X, ALU.add)
+            for r in range(ROWS):
+                nc.scalar.activation(squares[:], x_rows[:, r, :], ACT.Square, accum_out=row_sums[:, 1, r : r + 1])
+            nc.vector.tensor_scalar(row_means[:], row_sums[:], 1.0 / C, None, ALU.mult)
+            for start, count in SECOND:
+                for at in range(0, count, P):
+                    r = (start - HALF + at) // P
+                    for m in range(2):
+                        nc.tensor.matmul(
+                            moments[start][:, m, at : at + P],
+                            row_means[:, m, r : r + 1].to_broadcast([P, P]),
+                            ident_f32[:],
+                            start=False,
+                            stop=(at + P == count and m == 1),
+                            is_transpose=True,
+                        )
+
+        def statistics(start, count):
+            entries = slice(start, start + count)
+            mean_x, mean_xx = moments[start][:, 0, :], moments[start][:, 1, :]
+            mm = norm.tile([P, count], F32, name="mm")
+            nc.scalar.activation(mm[:], mean_x, ACT.Square)
+            nc.scalar.copy(mean[:, entries], mean_x)
+            var = norm.tile([P, count], F32, name="var")
+            nc.vector.tensor_tensor(var[:], mean_xx, mm[:], ALU.subtract)
+            nc.vector.tensor_scalar(var[:], var[:], 0.0, EPS, ALU.max, ALU.add)
+            nc.scalar.activation(rstd[:, entries], var[:], ACT.Abs_reciprocal_sqrt)
+
+        def normalise(b, start, count):
+            entries = slice(start, start + count)
+            f, at = divmod(start, HALF)
+            cen = norm.tile([P, count], F32, name="cen")
+            nc.vector.tensor_tensor(cen[:], xs[b][:, 0, entries], mean[:, entries], ALU.subtract)
+            nc.vector.tensor_tensor(cen[:], cen[:], rstd[:, entries], ALU.mult)
+            nc.scalar.activation(
+                h[f][b][:, at : at + count], cen[:], ACT.Identity, bias=beta_sb[:, b : b + 1], scale=gamma_sb[:, b : b + 1]
+            )
+
+        def project_v(f, tb):
+            sums = [psum.tile([P, HALF], F32, name=f"v_sum{part}", tag="acc") for part in range(C // VW)]
+            for b in range(CB):
+                for part in range(C // VW):
+                    nc.tensor.matmul(
+                        sums[part][:, :VW],
+                        h[f][b][:, tb * P : (tb + 1) * P],
+                        w_sb["v"][:, b, part * VW : (part + 1) * VW],
+                        start=(b == 0),
+                        stop=(b == CB - 1),
+                    )
+            nc.scalar.copy(v_t[f][tb][:, :VW], sums[0][:, :VW])
+            nc.vector.tensor_copy(v_t[f][tb][:, VW:], sums[1][:, :VW])
+
         with tc.tile_pool(name="table", bufs=1) as table:
             emb = [table.tile([P, V], F32, name=f"emb{b}") for b in range(CB)]
             for b in range(CB):
@@ -69,57 +156,26 @@ def tile_microgpttorch_b_kernel(tc, embedding, pos, gamma, beta, wq, wk, wv, wo,
             for name, w in (("v", wv), ("q", wq), ("k", wk), ("o", wo)):
                 nc.sync.dma_start(w_sb[name][:], w.rearrange("(b p) m -> p b m", p=P))
             for b in range(CB):
-                for s in range(B):
-                    nc.vector.tensor_tensor(
-                        xs[b][:, s, 0:T],
-                        emb[b][:].indirect(offsets[:, s * (T // 16) : (s + 1) * (T // 16)]),
-                        pos_sb[:, b, :],
-                        ALU.add,
-                    )
-                    nc.scalar.activation(xs[b][:, s, T : 2 * T], xs[b][:, s, 0:T], ACT.Square)
-                    nc.tensor.matmul(moments[s][:], mean_w[:], xs[b][:, s, :], start=(b == 0), stop=(b == CB - 1))
-
-        def statistics(s):
-            mm = norm.tile([P, T], F32, name="mm")
-            nc.scalar.activation(mm[:], moments[s][:, 0:T], ACT.Square)
-            nc.scalar.copy(mean[:, s, :], moments[s][:, 0:T])
-            var = norm.tile([P, T], F32, name="var")
-            nc.vector.tensor_tensor(var[:], moments[s][:, T : 2 * T], mm[:], ALU.subtract)
-            nc.vector.tensor_scalar(var[:], var[:], 0.0, EPS, ALU.max, ALU.add)
-            nc.scalar.activation(rstd[:, s, :], var[:], ACT.Abs_reciprocal_sqrt)
-
-        def normalise(b, first, count):
-            seqs = slice(first, first + count)
-            start = (first % SEQS) * T
-            cen = norm.tile([P, count, T], F32, name="cen")
-            nc.vector.tensor_tensor(cen[:], xs[b][:, seqs, 0:T], mean[:, seqs, :], ALU.subtract)
-            nc.vector.tensor_tensor(cen[:], cen[:], rstd[:, seqs, :], ALU.mult)
-            nc.scalar.activation(
-                h[first // SEQS][b][:, start : start + count * T].rearrange("p (s t) -> p s t", s=count),
-                cen[:], ACT.Identity, bias=beta_sb[:, b : b + 1], scale=gamma_sb[:, b : b + 1],
-            )
+                for start, count in UNITS if b == CB - 1 else UNITS + SECOND:
+                    look_up(b, start, count)
+                    add_moments(b, start, count)
+            for start, count in UNITS:
+                statistics(start, count)
+            for start, count in UNITS:
+                for b in range(CB):
+                    normalise(b, start, count)
+                if start < T:
+                    project_v(0, start // P)
+            last_block_of_second_half()
+            for start, count in SECOND:
+                statistics(start, count)
 
         with (
             tc.tile_pool(name="kept", bufs=1) as kept,
             tc.tile_pool(name="heads", bufs=3) as heads,
             tc.tile_pool(name="result", bufs=3) as result,
         ):
-            v_t = [[kept.tile([P, C], BF16, name=f"v_t{f}_{tb}") for tb in range(HALF // P)] for f in range(2)]
             attn = [[kept.tile([P, HALF], BF16, name=f"attn{f}_{a}") for a in range(H)] for f in range(2)]
-
-            def project_v(f, tb):
-                sums = [psum.tile([P, HALF], F32, name=f"v_sum{part}", tag="acc") for part in range(C // VW)]
-                for b in range(CB):
-                    for part in range(C // VW):
-                        nc.tensor.matmul(
-                            sums[part][:, :VW],
-                            h[f][b][:, tb * P : (tb + 1) * P],
-                            w_sb["v"][:, b, part * VW : (part + 1) * VW],
-                            start=(b == 0),
-                            stop=(b == CB - 1),
-                        )
-                nc.scalar.copy(v_t[f][tb][:, :VW], sums[0][:, :VW])
-                nc.vector.tensor_copy(v_t[f][tb][:, VW:], sums[1][:, :VW])
 
             def project_head(name, f, a):
                 acc = psum.tile([P, HALF], F32, name="acc")
@@ -203,30 +259,15 @@ def tile_microgpttorch_b_kernel(tc, embedding, pos, gamma, beta, wq, wk, wv, wo,
                         stop=(a == H - 1),
                     )
                 y = result.tile([P, HALF], F32, name="y")
-                nc.vector.tensor_tensor(
-                    y[:, :width].rearrange("p (s t) -> p s t", s=count),
-                    acc[:, :width].rearrange("p (s t) -> p s t", s=count),
-                    xs[b][:, f * SEQS + first : f * SEQS + first + count, 0:T],
-                    ALU.add,
-                )
                 start = f * HALF + first * T
+                nc.vector.tensor_tensor(y[:, :width], acc[:, :width], xs[b][:, 0, start : start + width], ALU.add)
                 nc.sync.dma_start(out[b * P : (b + 1) * P, start : start + width], y[:, :width])
 
             steps = [(f, a) for f in range(2) for a in range(H)]
             q, k, p, p_t = {}, {}, {}, {}
-            for s in range(SEQS):
-                statistics(s)
-            for s in range(SEQS):
-                for b in range(CB):
-                    normalise(b, s, 1)
-                if s == 0:
-                    project_v(0, 0)
-                    project_v(0, 1)
-            for s in range(SEQS, B):
-                statistics(s)
             for i in range(len(steps) + LAG):
                 if i < CB:
-                    normalise(i, SEQS, SEQS)
+                    normalise(i, HALF, HALF)
                 if i < len(steps):
                     q[i] = project_head("q", *steps[i])
                 else:

@@ -16,8 +16,7 @@ CB = C // P
 HALF = 512
 SEQS = HALF // T
 ROWS = HALF // P
-UNITS = [(0, P), (P, P), (T, T)]
-SECOND = [(HALF, T), (HALF + T, T)]
+RUNS = [(0, P), (P, P), (T, T), (HALF, T), (HALF + T, T)]
 VW = C // 2
 EPS = 1e-5
 NEG = -1.0e9
@@ -33,6 +32,7 @@ def tile_microgpttorch_b_kernel(tc, embedding, pos, gamma, beta, wq, wk, wv, wo,
     with (
         tc.tile_pool(name="held", bufs=1) as held,
         tc.tile_pool(name="norm", bufs=3) as norm,
+        tc.tile_pool(name="centred", bufs=6) as centred,
         tc.psum_pool(name="psum", bufs=4) as psum,
     ):
         offsets = held.tile([P, N // 16], U16, name="offsets")
@@ -43,8 +43,6 @@ def tile_microgpttorch_b_kernel(tc, embedding, pos, gamma, beta, wq, wk, wv, wo,
 
         ident = held.tile([P, P], BF16, name="ident")
         make_identity(nc, ident[:])
-        ident_f32 = held.tile([P, P], F32, name="ident_f32")
-        make_identity(nc, ident_f32[:])
         mean_w = held.tile([P, P], F32, name="mean_w")
         nc.vector.memset(mean_w[:], 1.0 / C)
         mask = held.tile([P, T], F32, name="mask")
@@ -58,18 +56,15 @@ def tile_microgpttorch_b_kernel(tc, embedding, pos, gamma, beta, wq, wk, wv, wo,
 
         xs = [held.tile([P, 2, N], F32, name=f"xs{b}") for b in range(CB)]
         h = [[held.tile([P, HALF], BF16, name=f"h{f}_{b}") for b in range(CB)] for f in range(2)]
-        row_sums = held.tile([P, 2, ROWS], F32, name="row_sums")
-        row_means = held.tile([P, 2, ROWS], F32, name="row_means")
-        squares = held.tile([P, P], F32, name="squares")
         mean = held.tile([P, N], F32, name="mean")
         rstd = held.tile([P, N], F32, name="rstd")
         w_sb = {name: held.tile([P, CB, C], BF16, name=f"w{name}_sb") for name in ("q", "k", "v", "o")}
         v_t = [[held.tile([P, C], BF16, name=f"v_t{f}_{tb}") for tb in range(ROWS)] for f in range(2)]
 
         moments = {}
-        for tag, runs in (("acc", UNITS), ("short", SECOND)):
-            for start, count in runs:
-                moments[start] = psum.tile([P, 2, count], F32, name=f"moments{start}", tag=tag)
+        for start, count in RUNS:
+            tag = "acc" if start < T else "short"
+            moments[start] = psum.tile([P, 2, count], F32, name=f"moments{start}", tag=tag)
 
         def look_up(b, start, count):
             nc.vector.tensor_tensor(
@@ -81,34 +76,14 @@ def tile_microgpttorch_b_kernel(tc, embedding, pos, gamma, beta, wq, wk, wv, wo,
 
         def add_moments(b, start, count):
             entries = slice(start, start + count)
-            nc.scalar.activation(xs[b][:, 1, entries], xs[b][:, 0, entries], ACT.Square)
-            nc.tensor.matmul(
-                moments[start][:], mean_w[:], xs[b][:, :, entries], start=(b == 0), stop=(b == CB - 1)
-            )
-
-        def last_block_of_second_half():
-            for start, count in SECOND:
-                look_up(CB - 1, start, count)
-            x_rows = psum.tile([P, ROWS, P], F32, name="x_rows", tag="short")
-            for r in range(ROWS):
-                at = HALF + r * P
-                nc.tensor.transpose(x_rows[:, r, :], xs[CB - 1][:, 0, at : at + P], ident_f32[:])
-            nc.vector.tensor_reduce(row_sums[:, 0, :], x_rows[:], AXIS.X, ALU.add)
-            for r in range(ROWS):
-                nc.scalar.activation(squares[:], x_rows[:, r, :], ACT.Square, accum_out=row_sums[:, 1, r : r + 1])
-            nc.vector.tensor_scalar(row_means[:], row_sums[:], 1.0 / C, None, ALU.mult)
-            for start, count in SECOND:
-                for at in range(0, count, P):
-                    r = (start - HALF + at) // P
-                    for m in range(2):
-                        nc.tensor.matmul(
-                            moments[start][:, m, at : at + P],
-                            row_means[:, m, r : r + 1].to_broadcast([P, P]),
-                            ident_f32[:],
-                            start=False,
-                            stop=(at + P == count and m == 1),
-                            is_transpose=True,
-                        )
+            if b < CB - 1:
+                nc.scalar.activation(xs[b][:, 1, entries], xs[b][:, 0, entries], ACT.Square)
+                nc.tensor.matmul(moments[start][:], mean_w[:], xs[b][:, :, entries], start=(b == 0), stop=False)
+                return
+            square = xs[b][:, 1, start % HALF : start % HALF + count]
+            nc.tensor.matmul(moments[start][:, 0, :], mean_w[:], xs[b][:, 0, entries], start=False, stop=False)
+            nc.scalar.activation(square, xs[b][:, 0, entries], ACT.Square)
+            nc.tensor.matmul(moments[start][:, 1, :], mean_w[:], square, start=False, stop=True)
 
         def statistics(start, count):
             entries = slice(start, start + count)
@@ -124,7 +99,7 @@ def tile_microgpttorch_b_kernel(tc, embedding, pos, gamma, beta, wq, wk, wv, wo,
         def normalise(b, start, count):
             entries = slice(start, start + count)
             f, at = divmod(start, HALF)
-            cen = norm.tile([P, count], F32, name="cen")
+            cen = centred.tile([P, count], F32, name="cen")
             nc.vector.tensor_tensor(cen[:], xs[b][:, 0, entries], mean[:, entries], ALU.subtract)
             nc.vector.tensor_tensor(cen[:], cen[:], rstd[:, entries], ALU.mult)
             nc.scalar.activation(
@@ -155,19 +130,26 @@ def tile_microgpttorch_b_kernel(tc, embedding, pos, gamma, beta, wq, wk, wv, wo,
                 nc.sync.dma_start(beta_sb[:], beta.rearrange("(b p) o -> p (b o)", p=P))
             for name, w in (("v", wv), ("q", wq), ("k", wk), ("o", wo)):
                 nc.sync.dma_start(w_sb[name][:], w.rearrange("(b p) m -> p b m", p=P))
-            for b in range(CB):
-                for start, count in UNITS if b == CB - 1 else UNITS + SECOND:
+            for b in range(CB - 1):
+                for start, count in RUNS:
                     look_up(b, start, count)
                     add_moments(b, start, count)
-            for start, count in UNITS:
+            for start, count in RUNS[:3]:
+                look_up(CB - 1, start, count)
+                add_moments(CB - 1, start, count)
+            for start, count in RUNS[:2]:
                 statistics(start, count)
-            for start, count in UNITS:
+            for start, count in RUNS[3:]:
+                look_up(CB - 1, start, count)
+                add_moments(CB - 1, start, count)
+            for start, count in RUNS[:3]:
+                if start >= T:
+                    statistics(start, count)
                 for b in range(CB):
                     normalise(b, start, count)
                 if start < T:
                     project_v(0, start // P)
-            last_block_of_second_half()
-            for start, count in SECOND:
+            for start, count in RUNS[3:]:
                 statistics(start, count)
 
         with (
@@ -177,12 +159,17 @@ def tile_microgpttorch_b_kernel(tc, embedding, pos, gamma, beta, wq, wk, wv, wo,
         ):
             attn = [[kept.tile([P, HALF], BF16, name=f"attn{f}_{a}") for a in range(H)] for f in range(2)]
 
-            def project_head(name, f, a):
+            def project_head(name, f, a, width=HALF):
                 acc = psum.tile([P, HALF], F32, name="acc")
-                for b in range(CB):
-                    nc.tensor.matmul(
-                        acc[:], w_sb[name][:, b, a * DH : (a + 1) * DH], h[f][b][:], start=(b == 0), stop=(b == CB - 1)
-                    )
+                for first in range(0, HALF, width):
+                    for b in range(CB):
+                        nc.tensor.matmul(
+                            acc[:, first : first + width],
+                            w_sb[name][:, b, a * DH : (a + 1) * DH],
+                            h[f][b][:, first : first + width],
+                            start=(b == 0),
+                            stop=(b == CB - 1),
+                        )
                 rounded = heads.tile([P, HALF], BF16, name=name)
                 nc.scalar.copy(rounded[:], acc[:])
                 return rounded
@@ -269,7 +256,8 @@ def tile_microgpttorch_b_kernel(tc, embedding, pos, gamma, beta, wq, wk, wv, wo,
                 if i < CB:
                     normalise(i, HALF, HALF)
                 if i < len(steps):
-                    q[i] = project_head("q", *steps[i])
+                    width = T if i == 0 else HALF
+                    q[i] = project_head("q", *steps[i], width)
                 else:
                     output_block(0, 2 * (i - len(steps)))
                 if i >= LAG:
@@ -277,7 +265,7 @@ def tile_microgpttorch_b_kernel(tc, embedding, pos, gamma, beta, wq, wk, wv, wo,
                 if 1 <= i <= len(steps):
                     p[i - 1] = softmax_weights(q[i - 1], k[i - 1])
                 if i < len(steps):
-                    k[i] = project_head("k", *steps[i])
+                    k[i] = project_head("k", *steps[i], width)
                 else:
                     output_block(0, 2 * (i - len(steps)) + 1)
                 if 2 <= i <= len(steps) + 1:

@@ -261,15 +261,15 @@ def tile_microgpttorch_b_kernel(tc, embedding, pos, gamma, beta, wq, wk, wv, wo,
                 else:
                     output_block(0, 2 * (i - len(steps)))
                 if i >= LAG:
-                    attend(*steps[i - LAG], p_t[i - LAG])
-                if 1 <= i <= len(steps):
-                    p[i - 1] = softmax_weights(q[i - 1], k[i - 1])
+                    p_t[i - LAG] = transpose_weights(*p[i - LAG])
                 if i < len(steps):
                     k[i] = project_head("k", *steps[i], width)
                 else:
                     output_block(0, 2 * (i - len(steps)) + 1)
-                if 2 <= i <= len(steps) + 1:
-                    p_t[i - 2] = transpose_weights(*p[i - 2])
+                if i >= LAG:
+                    attend(*steps[i - LAG], p_t[i - LAG])
+                if 1 <= i <= len(steps):
+                    p[i - 1] = softmax_weights(q[i - 1], k[i - 1])
                 if i < 2:
                     project_v(0, 2 + i)
                 if H - 1 <= i < H + LAG:

import math

import concourse.mybir as mybir
from concourse.masks import make_identity

F32 = mybir.dt.float32
BF16 = mybir.dt.bfloat16
U16 = mybir.dt.uint16
ALU = mybir.AluOpType
ACT = mybir.ActivationFunctionType
AXIS = mybir.AxisListType

P = 128
C, V, B, T, H, DH, N = 768, 4096, 4, 256, 6, 128, 1024
CB = C // P
HALF = 512
SEQS = HALF // T
ROWS = HALF // P
RUNS = [(0, P), (P, P), (T, T), (HALF, T), (HALF + T, T)]
VW = C // 2
EPS = 1e-5
NEG = -1.0e9
SCALE = 1.0 / math.sqrt(DH)
LAG = 3
assert 2 * LAG == CB

FLOPS = 4 * 2 * C * C * N + 2 * 2 * B * H * DH * (T * (T + 1) // 2)


def tile_microgpttorch_b_kernel(tc, embedding, pos, gamma, beta, wq, wk, wv, wo, offs, out):
    nc = tc.nc
    with (
        tc.tile_pool(name="held", bufs=1) as held,
        tc.tile_pool(name="norm", bufs=3) as norm,
        tc.tile_pool(name="centred", bufs=6) as centred,
        tc.psum_pool(name="psum", bufs=4) as psum,
    ):
        offsets = held.tile([P, N // 16], U16, name="offsets")
        nc.sync.dma_start(offsets[:], offs)
        pos_sb = held.tile([P, CB, T], F32, name="pos_sb")
        gamma_sb = held.tile([P, CB], F32, name="gamma_sb")
        beta_sb = held.tile([P, CB], F32, name="beta_sb")

        ident = held.tile([P, P], BF16, name="ident")
        make_identity(nc, ident[:])
        mean_w = held.tile([P, P], F32, name="mean_w")
        nc.vector.memset(mean_w[:], 1.0 / C)
        mask = held.tile([P, T], F32, name="mask")
        nc.gpsimd.memset(mask[:], 0.0)
        nc.gpsimd.affine_select(
            out=mask[:, P:T], in_=mask[:, P:T], pattern=[[-1, P]], compare_op=ALU.is_ge,
            fill=NEG, base=0, channel_multiplier=1,
        )
        warm = held.tile([P, 1], F32, name="warm")
        nc.scalar.activation(warm[:], mean_w[:, 0:1], ACT.Abs_reciprocal_sqrt)

        xs = [held.tile([P, 2, N], F32, name=f"xs{b}") for b in range(CB)]
        h = [[held.tile([P, HALF], BF16, name=f"h{f}_{b}") for b in range(CB)] for f in range(2)]
        mean = held.tile([P, N], F32, name="mean")
        rstd = held.tile([P, N], F32, name="rstd")
        w_sb = {name: held.tile([P, CB, C], BF16, name=f"w{name}_sb") for name in ("q", "k", "v", "o")}
        v_t = [[held.tile([P, C], BF16, name=f"v_t{f}_{tb}") for tb in range(ROWS)] for f in range(2)]

        moments = {}
        for start, count in RUNS:
            tag = "acc" if start < T else "short"
            moments[start] = psum.tile([P, 2, count], F32, name=f"moments{start}", tag=tag)

        def look_up(b, start, count):
            nc.vector.tensor_tensor(
                xs[b][:, 0, start : start + count],
                emb[b][:].indirect(offsets[:, start // 16 : (start + count) // 16]),
                pos_sb[:, b, start % T : start % T + count],
                ALU.add,
            )

        def add_moments(b, start, count):
            entries = slice(start, start + count)
            if b < CB - 1:
                nc.scalar.activation(xs[b][:, 1, entries], xs[b][:, 0, entries], ACT.Square)
                nc.tensor.matmul(moments[start][:], mean_w[:], xs[b][:, :, entries], start=(b == 0), stop=False)
                return
            square = xs[b][:, 1, start % HALF : start % HALF + count]
            nc.tensor.matmul(moments[start][:, 0, :], mean_w[:], xs[b][:, 0, entries], start=False, stop=False)
            nc.scalar.activation(square, xs[b][:, 0, entries], ACT.Square)
            nc.tensor.matmul(moments[start][:, 1, :], mean_w[:], square, start=False, stop=True)

        def statistics(start, count):
            entries = slice(start, start + count)
            mean_x, mean_xx = moments[start][:, 0, :], moments[start][:, 1, :]
            mm = norm.tile([P, count], F32, name="mm")
            nc.scalar.activation(mm[:], mean_x, ACT.Square)
            nc.scalar.copy(mean[:, entries], mean_x)
            var = norm.tile([P, count], F32, name="var")
            nc.vector.tensor_tensor(var[:], mean_xx, mm[:], ALU.subtract)
            nc.vector.tensor_scalar(var[:], var[:], 0.0, EPS, ALU.max, ALU.add)
            nc.scalar.activation(rstd[:, entries], var[:], ACT.Abs_reciprocal_sqrt)

        def normalise(b, start, count):
            entries = slice(start, start + count)
            f, at = divmod(start, HALF)
            cen = centred.tile([P, count], F32, name="cen")
            nc.vector.tensor_tensor(cen[:], xs[b][:, 0, entries], mean[:, entries], ALU.subtract)
            nc.vector.tensor_tensor(cen[:], cen[:], rstd[:, entries], ALU.mult)
            nc.scalar.activation(
                h[f][b][:, at : at + count], cen[:], ACT.Identity, bias=beta_sb[:, b : b + 1], scale=gamma_sb[:, b : b + 1]
            )

        def project_v(f, tb):
            sums = [psum.tile([P, HALF], F32, name=f"v_sum{part}", tag="acc") for part in range(C // VW)]
            for b in range(CB):
                for part in range(C // VW):
                    nc.tensor.matmul(
                        sums[part][:, :VW],
                        h[f][b][:, tb * P : (tb + 1) * P],
                        w_sb["v"][:, b, part * VW : (part + 1) * VW],
                        start=(b == 0),
                        stop=(b == CB - 1),
                    )
            nc.scalar.copy(v_t[f][tb][:, :VW], sums[0][:, :VW])
            nc.vector.tensor_copy(v_t[f][tb][:, VW:], sums[1][:, :VW])

        with tc.tile_pool(name="table", bufs=1) as table:
            emb = [table.tile([P, V], F32, name=f"emb{b}") for b in range(CB)]
            for b in range(CB):
                nc.sync.dma_start(pos_sb[:, b, :], pos[b * P : (b + 1) * P, :])
                nc.sync.dma_start(emb[b][:], embedding[b * P : (b + 1) * P, :])
            with nc.allow_non_contiguous_dma(reason="768 values, one to a partition in each of 6 columns"):
                nc.sync.dma_start(gamma_sb[:], gamma.rearrange("(b p) o -> p (b o)", p=P))
                nc.sync.dma_start(beta_sb[:], beta.rearrange("(b p) o -> p (b o)", p=P))
            for name, w in (("v", wv), ("q", wq), ("k", wk), ("o", wo)):
                nc.sync.dma_start(w_sb[name][:], w.rearrange("(b p) m -> p b m", p=P))
            for b in range(CB - 1):
                for start, count in RUNS:
                    look_up(b, start, count)
                    add_moments(b, start, count)
            for start, count in RUNS[:3]:
                look_up(CB - 1, start, count)
                add_moments(CB - 1, start, count)
            for start, count in RUNS[:2]:
                statistics(start, count)
            for start, count in RUNS[3:]:
                look_up(CB - 1, start, count)
                add_moments(CB - 1, start, count)
            for start, count in RUNS[:3]:
                if start >= T:
                    statistics(start, count)
                for b in range(CB):
                    normalise(b, start, count)
                if start < T:
                    project_v(0, start // P)
            for start, count in RUNS[3:]:
                statistics(start, count)

        with (
            tc.tile_pool(name="kept", bufs=1) as kept,
            tc.tile_pool(name="heads", bufs=3) as heads,
            tc.tile_pool(name="result", bufs=3) as result,
        ):
            attn = [[kept.tile([P, HALF], BF16, name=f"attn{f}_{a}") for a in range(H)] for f in range(2)]

            def project_head(name, f, a, width=HALF):
                acc = psum.tile([P, HALF], F32, name="acc")
                for first in range(0, HALF, width):
                    for b in range(CB):
                        nc.tensor.matmul(
                            acc[:, first : first + width],
                            w_sb[name][:, b, a * DH : (a + 1) * DH],
                            h[f][b][:, first : first + width],
                            start=(b == 0),
                            stop=(b == CB - 1),
                        )
                rounded = heads.tile([P, HALF], BF16, name=name)
                nc.scalar.copy(rounded[:], acc[:])
                return rounded

            def softmax_weights(q, k):
                sc_lo = psum.tile([P, SEQS, P], F32, name="sc_lo", tag="short")
                sc_hi = psum.tile([P, SEQS, T], F32, name="sc_hi", tag="short")
                for s in range(SEQS):
                    t0 = s * T
                    nc.tensor.matmul(sc_lo[:, s, :], q[:, t0 : t0 + P], k[:, t0 : t0 + P], start=True, stop=True)
                    nc.tensor.matmul(sc_hi[:, s, :], q[:, t0 + P : t0 + T], k[:, t0 : t0 + T], start=True, stop=True)
                e_lo = heads.tile([P, SEQS, P], F32, name="e_lo")
                e_hi = heads.tile([P, SEQS, T], F32, name="e_hi")
                nc.vector.scalar_tensor_tensor(
                    e_lo[:], sc_lo[:], SCALE, mask[:, P:T].unsqueeze(1).to_broadcast([P, SEQS, P]), ALU.mult, ALU.add
                )
                nc.vector.scalar_tensor_tensor(
                    e_hi[:], sc_hi[:], SCALE, mask[:].unsqueeze(1).to_broadcast([P, SEQS, T]), ALU.mult, ALU.add
                )
                neg_max = heads.tile([P, 2 * SEQS], F32, name="neg_max")
                nc.vector.tensor_reduce(neg_max[:, :SEQS], e_lo[:], AXIS.X, ALU.max, negate=True)
                nc.vector.tensor_reduce(neg_max[:, SEQS:], e_hi[:], AXIS.X, ALU.max, negate=True)
                total = heads.tile([P, 2 * SEQS], F32, name="total")
                for s in range(SEQS):
                    nc.scalar.activation(
                        e_lo[:, s, :], e_lo[:, s, :], ACT.Exp,
                        bias=neg_max[:, s : s + 1], accum_out=total[:, s : s + 1],
                    )
                    nc.scalar.activation(
                        e_hi[:, s, :], e_hi[:, s, :], ACT.Exp,
                        bias=neg_max[:, SEQS + s : SEQS + s + 1], accum_out=total[:, SEQS + s : SEQS + s + 1],
                    )
                inv = heads.tile([P, 2 * SEQS], F32, name="inv")
                nc.vector.reciprocal(inv[:], total[:])
                p_lo = heads.tile([P, SEQS, P], BF16, name="p_lo")
                p_hi = heads.tile([P, SEQS, T], BF16, name="p_hi")
                for s in range(SEQS):
                    nc.vector.tensor_scalar(p_lo[:, s, :], e_lo[:, s, :], inv[:, s : s + 1], None, ALU.mult)
                    nc.vector.tensor_scalar(p_hi[:, s, :], e_hi[:, s, :], inv[:, SEQS + s : SEQS + s + 1], None, ALU.mult)
                return p_lo, p_hi

            def transpose_weights(p_lo, p_hi):
                p_t_ps = psum.tile([P, SEQS, T + P], BF16, name="p_t_ps", tag="short")
                for s in range(SEQS):
                    nc.tensor.transpose(p_t_ps[:, s, 0:P], p_lo[:, s, :], ident[:])
                    nc.tensor.transpose(p_t_ps[:, s, P:T], p_hi[:, s, 0:P], ident[:])
                    nc.tensor.transpose(p_t_ps[:, s, T : T + P], p_hi[:, s, P:T], ident[:])
                p_t = heads.tile([P, SEQS, T + P], BF16, name="p_t")
                nc.vector.tensor_copy(p_t[:], p_t_ps[:])
                return p_t

            def attend(f, a, p_t):
                rows = slice(a * DH, (a + 1) * DH)
                at_ps = psum.tile([P, HALF], F32, name="at_ps", tag="short")
                for s in range(SEQS):
                    t0 = s * T
                    nc.tensor.matmul(
                        at_ps[:, t0 : t0 + T], v_t[f][2 * s][:, rows], p_t[:, s, 0:T], start=True, stop=False
                    )
                    nc.tensor.matmul(
                        at_ps[:, t0 + P : t0 + T], v_t[f][2 * s + 1][:, rows], p_t[:, s, T : T + P], start=False, stop=True
                    )
                nc.scalar.copy(attn[f][a][:], at_ps[:])

            def output_block(f, b, first=0, count=SEQS):
                width = count * T
                acc = psum.tile([P, HALF], F32, name="acc")
                for a in range(H):
                    nc.tensor.matmul(
                        acc[:, :width],
                        w_sb["o"][:, a, b * P : (b + 1) * P],
                        attn[f][a][:, first * T : first * T + width],
                        start=(a == 0),
                        stop=(a == H - 1),
                    )
                y = result.tile([P, HALF], F32, name="y")
                start = f * HALF + first * T
                nc.vector.tensor_tensor(y[:, :width], acc[:, :width], xs[b][:, 0, start : start + width], ALU.add)
                nc.sync.dma_start(out[b * P : (b + 1) * P, start : start + width], y[:, :width])

            steps = [(f, a) for f in range(2) for a in range(H)]
            q, k, p, p_t = {}, {}, {}, {}
            for i in range(len(steps) + LAG):
                if i < CB:
                    normalise(i, HALF, HALF)
                if i < len(steps):
                    width = T if i == 0 else HALF
                    q[i] = project_head("q", *steps[i], width)
                else:
                    output_block(0, 2 * (i - len(steps)))
                if i >= LAG:
                    p_t[i - LAG] = transpose_weights(*p[i - LAG])
                if i < len(steps):
                    k[i] = project_head("k", *steps[i], width)
                else:
                    output_block(0, 2 * (i - len(steps)) + 1)
                if i >= LAG:
                    attend(*steps[i - LAG], p_t[i - LAG])
                if 1 <= i <= len(steps):
                    p[i - 1] = softmax_weights(q[i - 1], k[i - 1])
                if i < 2:
                    project_v(0, 2 + i)
                if H - 1 <= i < H + LAG:
                    project_v(1, i - (H - 1))
            for b in range(CB - 1):
                output_block(1, b)
            for s in range(SEQS):
                output_block(1, CB - 1, s, 1)
